import numpy as np
import ml_dtypes


def mxq(x, axis, fmt="e4m3"):
    dtype, down = {"e4m3": (ml_dtypes.float8_e4m3fn, 7), "e5m2": (ml_dtypes.float8_e5m2, 14)}[fmt]
    v = np.moveaxis(np.asarray(x, np.float32).astype(ml_dtypes.bfloat16).astype(np.float64), axis, -1)
    blocks = v.reshape(v.shape[:-1] + (-1, 32))
    amax = np.abs(blocks).max(-1, keepdims=True)
    byte = np.maximum(np.where(amax > 0, np.frexp(amax)[1] - 1 + 127, 0) - down, 1)
    scale = np.exp2(byte - 127.0)
    codes = (blocks / scale).astype(np.float32).astype(dtype).astype(np.float64)
    return np.moveaxis((codes * scale).reshape(v.shape), -1, axis)


WIDE = False


def mx_kscale(k):
    if not WIDE:
        return np.ones(k)
    levels = np.array([10, -10, 5, -5, 0])
    a = np.random.permutation(np.resize(levels, k // 512 * 4)).reshape(k // 512, 4)
    idx = np.arange(k)
    return np.exp2(a[idx // 512, idx % 128 // 32])


BF16 = ml_dtypes.bfloat16


def bf(x):
    return np.asarray(x, np.float32).astype(BF16)


def f64(x):
    return np.asarray(x).astype(np.float64)


E2M1 = np.array([0.0, 0.5, 1.0, 1.5, 2.0, 3.0, 4.0, 6.0, -0.0, -0.5, -1.0, -1.5, -2.0, -3.0, -4.0, -6.0])


def pack_weight(w, fmt):
    k, n = w.shape
    w = f64(bf(w)).reshape(k // 32, 32, n)
    amax = np.abs(w).max(1)
    if fmt == "e4m3":
        byte = np.frexp(amax)[1] - 1 + 127 - 7
    else:
        mant, ex = np.frexp(amax / 6.0)
        byte = np.where(mant > 0.5, ex, ex - 1) + 127
    byte = np.clip(np.where(amax > 0, byte, 1), 1, 254)
    scaled = (w * np.exp2(127.0 - byte)[:, None, :]).reshape(k, n).astype(np.float32)
    by_word = np.ascontiguousarray(scaled.reshape(k // 512, 128, 4, n).transpose(0, 1, 3, 2))
    if fmt == "e4m3":
        words = by_word.astype(ml_dtypes.float8_e4m3fn).view(np.uint8)
    else:
        c = by_word.astype(ml_dtypes.float4_e2m1fn).view(np.uint8) & 0xF
        words = c[..., 0::2] | (c[..., 1::2] << 4)
    return np.ascontiguousarray(words), np.ascontiguousarray(byte.astype(np.uint8).reshape(k // 512, 16, n))


def unpack_weight(words, scales, fmt):
    g, p, n, _ = words.shape
    if fmt == "e4m3":
        vals = np.ascontiguousarray(words).view(ml_dtypes.float8_e4m3fn).astype(np.float64)
    else:
        nib = np.empty((g, p, n, 4), np.uint8)
        nib[..., 0::2] = words & 0xF
        nib[..., 1::2] = words >> 4
        vals = E2M1[nib]
    vals = vals * np.repeat(np.exp2(scales.astype(np.float64) - 127.0), 8, axis=1)[..., None]
    return vals.transpose(0, 1, 3, 2).reshape(g * 512, n)


N, M, P, D = 128, 4096, 4096, 16
LN_EPS = 1e-5
LENGTHSCALE = 1.0
INPUT_LB, INPUT_UB = -2.0, 2.0


def setup_inputs():
    s = mx_kscale(M)
    r = s.max() / s
    c = np.random.standard_normal(D)
    c = (c - c.mean()) / c.std()
    x = c + np.random.standard_normal((N, D)) * 1.6 / D
    z = c + np.random.uniform(INPUT_LB, INPUT_UB, (M, D)) * 1.6 / D
    z[:, 0] += np.log(r) * LENGTHSCALE
    g = np.random.standard_normal((M, P)) * 4.0 / np.sqrt(M)
    w = np.triu(g) + 0.1 * np.tril(g, -1) + np.eye(M, P)
    words, scales = pack_weight(w * r[:, None], "e4m3")
    return {"x": bf(x), "design_points": bf(z), "chol_inv_words": words, "chol_inv_scales": scales}


def reference(x, design_points, chol_inv_words, chol_inv_scales):
    x, z = f64(x), f64(design_points)
    mean = np.mean(x, axis=-1, keepdims=True)
    var = np.mean(np.square(x - mean), axis=-1, keepdims=True)
    xn = (x - mean) / np.sqrt(var + LN_EPS)
    l1 = np.zeros((N, M))
    for d in range(D):
        l1 = l1 + np.abs(xn[:, d, None] - z[None, :, d])
    kmat = np.exp(-l1 / LENGTHSCALE)
    return mxq(kmat, 1, "e4m3") @ unpack_weight(chol_inv_words, chol_inv_scales, "e4m3")

@@ -1,0 +1,227 @@
+from contextlib import ExitStack
+
+import concourse.mybir as mybir
+from concourse.masks import make_identity
+
+F32 = mybir.dt.float32
+BF16 = mybir.dt.bfloat16
+I32 = mybir.dt.int32
+U8 = mybir.dt.uint8
+U32 = mybir.dt.uint32
+FP8X4 = mybir.dt.float8_e4m3fn_x4
+ACT = mybir.ActivationFunctionType
+ALU = mybir.AluOpType
+AX = mybir.AxisListType
+
+P = 128
+D = 16
+G = 8
+T = 4
+COLS = 4096
+CHUNK = 512
+N_CHUNKS = COLS // CHUNK
+LN_EPS = 1e-5
+S_TERMS = 7
+EARLY_CHUNKS = 6
+
+FLOPS = 2 * 128 * 4096 * 4096
+
+
+def tile_tmk_w_kernel(tc, x, design_points, chol_inv_words, chol_inv_scales, out):
+    nc = tc.nc
+    with ExitStack() as ctx:
+        const = ctx.enter_context(tc.tile_pool(name="const", bufs=1))
+        wpool = ctx.enter_context(tc.tile_pool(name="wpool", bufs=1))
+        terms = ctx.enter_context(tc.tile_pool(name="terms", bufs=12))
+        chains = ctx.enter_context(tc.tile_pool(name="chains", bufs=2))
+        stage = ctx.enter_context(tc.tile_pool(name="stage", bufs=2))
+        outp = ctx.enter_context(tc.tile_pool(name="outp", bufs=4))
+        psum = ctx.enter_context(tc.psum_pool(name="psum", bufs=1))
+
+        x_sb = const.tile([P, D], BF16, name="x_sb")
+        nc.sync.dma_start(out=x_sb[:], in_=x)
+        z_sb = const.tile([P, G, T * D], BF16, name="z_sb")
+        with nc.allow_non_contiguous_dma(reason="128-byte runs of design points"):
+            nc.sync.dma_start(
+                out=z_sb[:],
+                in_=design_points.rearrange("(g p t) d -> p g (t d)", g=G, p=P, t=T),
+            )
+        w_scales = const.tile([P, 2, COLS], U8, name="w_scales", align_bytes=64)
+        nc.vector.memset(w_scales[:].bitcast(I32), 0)
+        for half in range(2):
+            for q in range(4):
+                nc.sync.dma_start(
+                    out=w_scales[32 * q : 32 * q + 16, half, :].bitcast(I32),
+                    in_=chol_inv_scales[4 * half : 4 * half + 4, 4 * q : 4 * q + 4, :].bitcast(I32),
+                )
+        w_words = []
+        for g in range(G):
+            wt = wpool.tile([P, 4 * COLS], U8, name="w%d" % g, align_bytes=64)
+            nc.sync.dma_start(
+                out=wt[:].bitcast(I32),
+                in_=chol_inv_words[g].rearrange("p n t -> p (n t)").bitcast(I32),
+            )
+            w_words.append(wt)
+
+        ident_f = const.tile([P, P], F32, name="ident_f")
+        make_identity(nc, ident_f[:])
+        ident_b = const.tile([P, P], BF16, name="ident_b")
+        make_identity(nc, ident_b[:])
+
+        xf = const.tile([P, D], F32, name="xf")
+        nc.vector.tensor_copy(out=xf[:], in_=x_sb[:])
+        stats = const.tile([P, 6], F32, name="stats")
+        nc.vector.bn_stats(out=stats[:], in_=xf[:])
+        mv = const.tile([P, 2], F32, name="mv")
+        nc.vector.bn_aggr(out=mv[:], in_=stats[:])
+        vare = const.tile([P, 1], F32, name="vare")
+        nc.vector.tensor_scalar_add(out=vare[:], in0=mv[:, 1:2], scalar1=LN_EPS)
+        std = const.tile([P, 1], F32, name="std")
+        nc.scalar.activation(out=std[:], in_=vare[:], func=ACT.Sqrt)
+        rstd = const.tile([P, 1], F32, name="rstd")
+        nc.vector.reciprocal(out=rstd[:], in_=std[:])
+        xn = const.tile([P, D], F32, name="xn")
+        nc.vector.tensor_scalar(
+            out=xn[:], in0=xf[:], scalar1=mv[:, 0:1], scalar2=rstd[:], op0=ALU.subtract, op1=ALU.mult
+        )
+        exp_bias = const.tile([P, 1], F32, name="exp_bias")
+        nc.vector.tensor_reduce(out=exp_bias[:], in_=xn[:, S_TERMS:D], axis=AX.X, op=ALU.add)
+
+        xnb = const.tile([P, D, P], F32, name="xnb")
+        for k in (0, 2, 1, 3):
+            bc = psum.tile([P, 4, P], F32, tag="acc%d" % k, name="bc%d" % k)
+            for j in range(4):
+                d = 4 * k + j
+                nc.tensor.transpose(
+                    out=bc[:, j, :], in_=xn[:, d : d + 1].to_broadcast([P, P]), identity=ident_f[:]
+                )
+            if k < 2:
+                nc.scalar.copy(out=xnb[:, 4 * k : 4 * k + 4, :], in_=bc[:])
+            else:
+                nc.vector.tensor_copy(out=xnb[:, 4 * k : 4 * k + 4, :], in_=bc[:])
+
+        zf = const.tile([P, G * T * D], F32, name="zf")
+        nc.vector.tensor_copy(out=zf[:], in_=z_sb[:].rearrange("p g k -> p (g k)"))
+        zh = const.tile([P, G * T * D], F32, name="zh")
+        nc.vector.tensor_scalar_mul(out=zh[:], in0=zf[:], scalar1=-0.5)
+        kc = const.tile([P, G * T], F32, name="kc")
+        nc.vector.tensor_reduce(
+            out=kc[:],
+            in_=zh[:].rearrange("p (b d) -> p b d", d=D)[:, :, S_TERMS:D],
+            axis=AX.X,
+            op=ALU.add,
+        )
+
+        kcodes = const.tile([P, G, P], U32, name="kcodes", align_bytes=64)
+        kscales = const.tile([P, G, P], U8, name="kscales", align_bytes=64)
+
+        work_tags = ("wka", "wkb")
+        v_dims = [d for d in range(8, D)] + [d for d in range(S_TERMS, 8)]
+        acc = {}
+
+        def mx_pass(c, g):
+            k4 = 4 * (g % 4)
+            nc.tensor.matmul_mx(
+                out=acc[c][:],
+                lhsT=kcodes[:, g, :].bitcast(FP8X4),
+                lhsT_scale=kscales[:, g, :],
+                rhs=w_words[g][:, 4 * CHUNK * c : 4 * CHUNK * (c + 1)].bitcast(FP8X4),
+                rhs_scale=w_scales[k4:P, g // 4, CHUNK * c : CHUNK * (c + 1)],
+                start=(g == 0),
+                stop=(g == G - 1),
+            )
+
+        def evacuate(c):
+            res = outp.tile([P, CHUNK], F32, tag="res", name="res%d" % c)
+            if c % 2 == 0:
+                nc.vector.tensor_copy(out=res[:], in_=acc[c][:])
+            else:
+                nc.scalar.copy(out=res[:], in_=acc[c][:])
+            nc.sync.dma_start(out=out[:, CHUNK * c : CHUNK * (c + 1)], in_=res[:])
+
+        for g in range(G):
+            l1 = psum.tile([P, T * P], F32, tag=work_tags[g % 2], name="l1_%d" % g)
+            first = True
+            for t in range(T):
+                b = g * T + t
+                for d in range(S_TERMS):
+                    term = terms.tile([P, P], F32, tag="term", name="term")
+                    nc.scalar.activation(
+                        out=term[:],
+                        in_=xnb[:, d, :],
+                        func=ACT.Abs,
+                        bias=zh[:, b * D + d : b * D + d + 1],
+                        scale=0.5,
+                    )
+                    nc.tensor.matmul(
+                        out=l1[:, t * P : (t + 1) * P],
+                        lhsT=term[:],
+                        rhs=ident_f[:],
+                        is_transpose=True,
+                        start=first,
+                        stop=False,
+                    )
+                    first = False
+            sums = []
+            for t in range(T):
+                sums.append(chains.tile([P, P], F32, tag="sum%d" % t, name="sum%d" % t))
+            for k, d in enumerate(v_dims):
+                for t in range(T):
+                    b = g * T + t
+                    if k == 0:
+                        nc.vector.tensor_scalar(
+                            out=sums[t][:],
+                            in0=xnb[:, d, :],
+                            scalar1=zf[:, b * D + d : b * D + d + 1],
+                            scalar2=kc[:, b : b + 1],
+                            op0=ALU.max,
+                            op1=ALU.add,
+                        )
+                    else:
+                        nc.vector.scalar_tensor_tensor(
+                            out=sums[t][:],
+                            in0=xnb[:, d, :],
+                            scalar=zf[:, b * D + d : b * D + d + 1],
+                            in1=sums[t][:],
+                            op0=ALU.max,
+                            op1=ALU.add,
+                        )
+            for t in range(T):
+                nc.tensor.matmul(
+                    out=l1[:, t * P : (t + 1) * P],
+                    lhsT=sums[t][:],
+                    rhs=ident_f[:],
+                    is_transpose=True,
+                    start=False,
+                    stop=(t == T - 1),
+                )
+
+            kn = stage.tile([P, T * P], BF16, tag="kn", name="kn")
+            nc.scalar.activation(out=kn[:], in_=l1[:], func=ACT.Exp, bias=exp_bias[:], scale=-2.0)
+            xt = psum.tile([P, T, P], BF16, tag=work_tags[g % 2], name="xt_%d" % g)
+            for t in range(T):
+                nc.tensor.transpose(out=xt[:, t, :], in_=kn[:, t * P : (t + 1) * P], identity=ident_b[:])
+            grouped = stage.tile([P, P, T], BF16, tag="grouped", name="grouped", align_bytes=64)
+            nc.scalar.copy(out=grouped[:], in_=xt[:].rearrange("p t n -> p n t"))
+            nc.vector.quantize_mx(
+                out=kcodes[:, g, :].bitcast(FP8X4),
+                scales=kscales[:, g, :],
+                in_=grouped[:].rearrange("p n t -> p (n t)"),
+            )
+            if g == 0:
+                for c in range(EARLY_CHUNKS):
+                    acc[c] = psum.tile([P, CHUNK], F32, tag="acc%d" % c, name="out%d" % c)
+            for c in range(EARLY_CHUNKS):
+                mx_pass(c, g)
+            if g == G - 2:
+                acc[6] = psum.tile([P, CHUNK], F32, tag=work_tags[g % 2], name="out6")
+                for gg in range(G - 1):
+                    mx_pass(6, gg)
+            if g == G - 1:
+                mx_pass(6, g)
+                for c in range(EARLY_CHUNKS + 1):
+                    evacuate(c)
+                acc[7] = psum.tile([P, CHUNK], F32, tag=work_tags[g % 2], name="out7")
+                for gg in range(G):
+                    mx_pass(7, gg)
+                evacuate(7)

@@ -19,10 +19,11 @@ G = 8
 T = 4
 COLS = 4096
 CHUNK = 512
-N_CHUNKS = COLS // CHUNK
 LN_EPS = 1e-5
 S_TERMS = 7
 EARLY_CHUNKS = 6
+MX_AFTER = (6, 18, 30)
+V_SPLIT = 24
 
 FLOPS = 2 * 128 * 4096 * 4096
 
@@ -30,12 +31,13 @@ FLOPS = 2 * 128 * 4096 * 4096
 def tile_tmk_w_kernel(tc, x, design_points, chol_inv_words, chol_inv_scales, out):
     nc = tc.nc
     with ExitStack() as ctx:
+        ctx.enter_context(tc.manual_schedule())
         const = ctx.enter_context(tc.tile_pool(name="const", bufs=1))
         wpool = ctx.enter_context(tc.tile_pool(name="wpool", bufs=1))
-        terms = ctx.enter_context(tc.tile_pool(name="terms", bufs=12))
+        terms = ctx.enter_context(tc.tile_pool(name="terms", bufs=16))
         chains = ctx.enter_context(tc.tile_pool(name="chains", bufs=2))
         stage = ctx.enter_context(tc.tile_pool(name="stage", bufs=2))
-        outp = ctx.enter_context(tc.tile_pool(name="outp", bufs=4))
+        outp = ctx.enter_context(tc.tile_pool(name="outp", bufs=8))
         psum = ctx.enter_context(tc.psum_pool(name="psum", bufs=1))
 
         x_sb = const.tile([P, D], BF16, name="x_sb")
@@ -63,45 +65,42 @@ def tile_tmk_w_kernel(tc, x, design_points, chol_inv_words, chol_inv_scales, out
             )
             w_words.append(wt)
 
+        neg_half = const.tile([P, 1], F32, name="neg_half")
+        nc.gpsimd.memset(neg_half[:], -0.5)
+        scratch = const.tile([P, 1], F32, name="scratch")
+        nc.gpsimd.memset(scratch[:], 0.0)
+        scratch2 = const.tile([P, 1], F32, name="scratch2")
+        nc.scalar.activation(out=scratch2[:], in_=scratch[:], func=ACT.Exp)
         ident_f = const.tile([P, P], F32, name="ident_f")
         make_identity(nc, ident_f[:])
         ident_b = const.tile([P, P], BF16, name="ident_b")
         make_identity(nc, ident_b[:])
 
-        xf = const.tile([P, D], F32, name="xf")
-        nc.vector.tensor_copy(out=xf[:], in_=x_sb[:])
         stats = const.tile([P, 6], F32, name="stats")
-        nc.vector.bn_stats(out=stats[:], in_=xf[:])
+        nc.vector.bn_stats(out=stats[:], in_=x_sb[:])
         mv = const.tile([P, 2], F32, name="mv")
         nc.vector.bn_aggr(out=mv[:], in_=stats[:])
         vare = const.tile([P, 1], F32, name="vare")
         nc.vector.tensor_scalar_add(out=vare[:], in0=mv[:, 1:2], scalar1=LN_EPS)
-        std = const.tile([P, 1], F32, name="std")
-        nc.scalar.activation(out=std[:], in_=vare[:], func=ACT.Sqrt)
         rstd = const.tile([P, 1], F32, name="rstd")
-        nc.vector.reciprocal(out=rstd[:], in_=std[:])
+        nc.gpsimd.tensor_tensor(out=rstd[:], in0=vare[:], in1=neg_half[:], op=ALU.pow)
+        zf = const.tile([P, G * T * D], F32, name="zf")
+        nc.vector.tensor_copy(out=zf[:], in_=z_sb[:].rearrange("p g k -> p (g k)"))
         xn = const.tile([P, D], F32, name="xn")
         nc.vector.tensor_scalar(
-            out=xn[:], in0=xf[:], scalar1=mv[:, 0:1], scalar2=rstd[:], op0=ALU.subtract, op1=ALU.mult
+            out=xn[:], in0=x_sb[:], scalar1=mv[:, 0:1], scalar2=rstd[:], op0=ALU.subtract, op1=ALU.mult
         )
-        exp_bias = const.tile([P, 1], F32, name="exp_bias")
-        nc.vector.tensor_reduce(out=exp_bias[:], in_=xn[:, S_TERMS:D], axis=AX.X, op=ALU.add)
 
         xnb = const.tile([P, D, P], F32, name="xnb")
+        spread = {}
         for k in (0, 2, 1, 3):
-            bc = psum.tile([P, 4, P], F32, tag="acc%d" % k, name="bc%d" % k)
+            spread[k] = psum.tile([P, 4, P], F32, tag="acc%d" % k, name="bc%d" % k)
             for j in range(4):
                 d = 4 * k + j
                 nc.tensor.transpose(
-                    out=bc[:, j, :], in_=xn[:, d : d + 1].to_broadcast([P, P]), identity=ident_f[:]
+                    out=spread[k][:, j, :], in_=xn[:, d : d + 1].to_broadcast([P, P]), identity=ident_f[:]
                 )
-            if k < 2:
-                nc.scalar.copy(out=xnb[:, 4 * k : 4 * k + 4, :], in_=bc[:])
-            else:
-                nc.vector.tensor_copy(out=xnb[:, 4 * k : 4 * k + 4, :], in_=bc[:])
 
-        zf = const.tile([P, G * T * D], F32, name="zf")
-        nc.vector.tensor_copy(out=zf[:], in_=z_sb[:].rearrange("p g k -> p (g k)"))
         zh = const.tile([P, G * T * D], F32, name="zh")
         nc.vector.tensor_scalar_mul(out=zh[:], in0=zf[:], scalar1=-0.5)
         kc = const.tile([P, G * T], F32, name="kc")
@@ -111,6 +110,11 @@ def tile_tmk_w_kernel(tc, x, design_points, chol_inv_words, chol_inv_scales, out
             axis=AX.X,
             op=ALU.add,
         )
+        exp_bias = const.tile([P, 1], F32, name="exp_bias")
+        nc.vector.tensor_reduce(out=exp_bias[:], in_=xn[:, S_TERMS:D], axis=AX.X, op=ALU.add)
+        nc.scalar.copy(out=xnb[:, 0:4, :], in_=spread[0][:])
+        nc.vector.tensor_copy(out=xnb[:, 8:12, :], in_=spread[2][:])
+        nc.vector.tensor_copy(out=xnb[:, 12:16, :], in_=spread[3][:])
 
         kcodes = const.tile([P, G, P], U32, name="kcodes", align_bytes=64)
         kscales = const.tile([P, G, P], U8, name="kscales", align_bytes=64)
@@ -118,6 +122,16 @@ def tile_tmk_w_kernel(tc, x, design_points, chol_inv_words, chol_inv_scales, out
         work_tags = ("wka", "wkb")
         v_dims = [d for d in range(8, D)] + [d for d in range(S_TERMS, 8)]
         acc = {}
+        l1 = {}
+        sums = {}
+        kn = {}
+        xt = {}
+        grouped = {}
+        opened = {}
+        t_count = [0]
+        pending = []
+        late = []
+        pos = [0, 0]
 
         def mx_pass(c, g):
             k4 = 4 * (g % 4)
@@ -131,6 +145,100 @@ def tile_tmk_w_kernel(tc, x, design_points, chol_inv_words, chol_inv_scales, out
                 stop=(g == G - 1),
             )
 
+        def emit_passes(n):
+            for i in range(n):
+                if pos[0] < len(pending):
+                    c, g = pending[pos[0]]
+                    pos[0] += 1
+                    mx_pass(c, g)
+                elif pos[1] < len(late):
+                    c, g = late[pos[1]]
+                    pos[1] += 1
+                    mx_pass(c, g)
+
+        def after_t():
+            t_count[0] += 1
+            if t_count[0] in MX_AFTER:
+                emit_passes(2)
+
+        def add_transposed(g, t, src, last):
+            nc.tensor.matmul(
+                out=l1[g][:, t * P : (t + 1) * P],
+                lhsT=src,
+                rhs=ident_f[:],
+                is_transpose=True,
+                start=(g not in opened),
+                stop=last,
+            )
+            opened[g] = True
+            after_t()
+
+        def scalar_terms(g, pairs):
+            for t, d in pairs:
+                b = g * T + t
+                term = terms.tile([P, P], F32, tag="term", name="term")
+                nc.scalar.activation(
+                    out=term[:],
+                    in_=xnb[:, d, :],
+                    func=ACT.Abs,
+                    bias=zh[:, b * D + d : b * D + d + 1],
+                    scale=0.5,
+                )
+                add_transposed(g, t, term[:], False)
+
+        def vector_ops(g, lo, hi):
+            for i in range(lo, hi):
+                k = i // T
+                t = i % T
+                d = v_dims[k]
+                b = g * T + t
+                if k == 0:
+                    sums[(g, t)] = chains.tile([P, P], F32, tag="sum%d" % t, name="sum%d" % t)
+                    nc.vector.tensor_scalar(
+                        out=sums[(g, t)][:],
+                        in0=xnb[:, d, :],
+                        scalar1=zf[:, b * D + d : b * D + d + 1],
+                        scalar2=kc[:, b : b + 1],
+                        op0=ALU.max,
+                        op1=ALU.add,
+                    )
+                else:
+                    nc.vector.scalar_tensor_tensor(
+                        out=sums[(g, t)][:],
+                        in0=xnb[:, d, :],
+                        scalar=zf[:, b * D + d : b * D + d + 1],
+                        in1=sums[(g, t)][:],
+                        op0=ALU.max,
+                        op1=ALU.add,
+                    )
+
+        def vector_sums_in(g):
+            for t in range(T):
+                add_transposed(g, t, sums[(g, t)][:], t == T - 1)
+
+        def exponent(g):
+            kn[g] = stage.tile([P, T * P], BF16, tag="kn", name="kn")
+            nc.scalar.activation(out=kn[g][:], in_=l1[g][:], func=ACT.Exp, bias=exp_bias[:], scale=-2.0)
+
+        def turn_back(g):
+            xt[g] = psum.tile([P, T, P], BF16, tag=work_tags[g % 2], name="xt_%d" % g)
+            for t in range(T):
+                nc.tensor.transpose(
+                    out=xt[g][:, t, :], in_=kn[g][:, t * P : (t + 1) * P], identity=ident_b[:]
+                )
+                after_t()
+
+        def regroup(g):
+            grouped[g] = stage.tile([P, P, T], BF16, tag="grouped", name="grouped", align_bytes=64)
+            nc.scalar.copy(out=grouped[g][:], in_=xt[g][:].rearrange("p t n -> p n t"))
+
+        def quantise(g):
+            nc.vector.quantize_mx(
+                out=kcodes[:, g, :].bitcast(FP8X4),
+                scales=kscales[:, g, :],
+                in_=grouped[g][:].rearrange("p n t -> p (n t)"),
+            )
+
         def evacuate(c):
             res = outp.tile([P, CHUNK], F32, tag="res", name="res%d" % c)
             if c % 2 == 0:
@@ -139,89 +247,62 @@ def tile_tmk_w_kernel(tc, x, design_points, chol_inv_words, chol_inv_scales, out
                 nc.scalar.copy(out=res[:], in_=acc[c][:])
             nc.sync.dma_start(out=out[:, CHUNK * c : CHUNK * (c + 1)], in_=res[:])
 
+        n_vops = T * len(v_dims)
         for g in range(G):
-            l1 = psum.tile([P, T * P], F32, tag=work_tags[g % 2], name="l1_%d" % g)
-            first = True
-            for t in range(T):
-                b = g * T + t
-                for d in range(S_TERMS):
-                    term = terms.tile([P, P], F32, tag="term", name="term")
-                    nc.scalar.activation(
-                        out=term[:],
-                        in_=xnb[:, d, :],
-                        func=ACT.Abs,
-                        bias=zh[:, b * D + d : b * D + d + 1],
-                        scale=0.5,
-                    )
-                    nc.tensor.matmul(
-                        out=l1[:, t * P : (t + 1) * P],
-                        lhsT=term[:],
-                        rhs=ident_f[:],
-                        is_transpose=True,
-                        start=first,
-                        stop=False,
-                    )
-                    first = False
-            sums = []
-            for t in range(T):
-                sums.append(chains.tile([P, P], F32, tag="sum%d" % t, name="sum%d" % t))
-            for k, d in enumerate(v_dims):
-                for t in range(T):
-                    b = g * T + t
-                    if k == 0:
-                        nc.vector.tensor_scalar(
-                            out=sums[t][:],
-                            in0=xnb[:, d, :],
-                            scalar1=zf[:, b * D + d : b * D + d + 1],
-                            scalar2=kc[:, b : b + 1],
-                            op0=ALU.max,
-                            op1=ALU.add,
-                        )
-                    else:
-                        nc.vector.scalar_tensor_tensor(
-                            out=sums[t][:],
-                            in0=xnb[:, d, :],
-                            scalar=zf[:, b * D + d : b * D + d + 1],
-                            in1=sums[t][:],
-                            op0=ALU.max,
-                            op1=ALU.add,
-                        )
-            for t in range(T):
-                nc.tensor.matmul(
-                    out=l1[:, t * P : (t + 1) * P],
-                    lhsT=sums[t][:],
-                    rhs=ident_f[:],
-                    is_transpose=True,
-                    start=False,
-                    stop=(t == T - 1),
-                )
-
-            kn = stage.tile([P, T * P], BF16, tag="kn", name="kn")
-            nc.scalar.activation(out=kn[:], in_=l1[:], func=ACT.Exp, bias=exp_bias[:], scale=-2.0)
-            xt = psum.tile([P, T, P], BF16, tag=work_tags[g % 2], name="xt_%d" % g)
-            for t in range(T):
-                nc.tensor.transpose(out=xt[:, t, :], in_=kn[:, t * P : (t + 1) * P], identity=ident_b[:])
-            grouped = stage.tile([P, P, T], BF16, tag="grouped", name="grouped", align_bytes=64)
-            nc.scalar.copy(out=grouped[:], in_=xt[:].rearrange("p t n -> p n t"))
-            nc.vector.quantize_mx(
-                out=kcodes[:, g, :].bitcast(FP8X4),
-                scales=kscales[:, g, :],
-                in_=grouped[:].rearrange("p n t -> p (n t)"),
-            )
+            t_count[0] = 0
+            l1[g] = psum.tile([P, T * P], F32, tag=work_tags[g % 2], name="l1_%d" % g)
             if g == 0:
+                scalar_terms(g, [(t, d) for t in (0, 1) for d in range(4)])
+                nc.scalar.copy(out=xnb[:, 4:8, :], in_=spread[1][:])
+                scalar_terms(g, [(t, d) for t in (0, 1) for d in range(4, S_TERMS)])
+                vector_ops(g, 0, V_SPLIT)
+            else:
+                vector_sums_in(g - 1)
+                scalar_terms(g, [(0, d) for d in range(S_TERMS)])
+                exponent(g - 1)
+                turn_back(g - 1)
+                scalar_terms(g, [(1, d) for d in range(S_TERMS)])
+                regroup(g - 1)
+                if g - 1 == G - 2:
+                    acc[6] = psum.tile([P, CHUNK], F32, tag=work_tags[(g - 1) % 2], name="out6")
+                    for gg in range(G - 2):
+                        late.append((6, gg))
+                vector_ops(g, 0, V_SPLIT)
+                quantise(g - 1)
+                if g - 1 == 0:
+                    for c in range(EARLY_CHUNKS):
+                        acc[c] = psum.tile([P, CHUNK], F32, tag="acc%d" % c, name="out%d" % c)
                 for c in range(EARLY_CHUNKS):
-                    acc[c] = psum.tile([P, CHUNK], F32, tag="acc%d" % c, name="out%d" % c)
-            for c in range(EARLY_CHUNKS):
-                mx_pass(c, g)
-            if g == G - 2:
-                acc[6] = psum.tile([P, CHUNK], F32, tag=work_tags[g % 2], name="out6")
-                for gg in range(G - 1):
-                    mx_pass(6, gg)
-            if g == G - 1:
-                mx_pass(6, g)
-                for c in range(EARLY_CHUNKS + 1):
-                    evacuate(c)
-                acc[7] = psum.tile([P, CHUNK], F32, tag=work_tags[g % 2], name="out7")
-                for gg in range(G):
-                    mx_pass(7, gg)
-                evacuate(7)
+                    pending.append((c, g - 1))
+                if g - 1 == G - 2:
+                    late.append((6, g - 1))
+            scalar_terms(g, [(2, d) for d in range(S_TERMS)])
+            scalar_terms(g, [(3, d) for d in range(S_TERMS)])
+            vector_ops(g, V_SPLIT, n_vops)
+
+        g = G - 1
+        t_count[0] = 100
+        vector_sums_in(g)
+        emit_passes(3)
+        exponent(g)
+        turn_back(g)
+        emit_passes(4)
+        regroup(g)
+        quantise(g)
+        acc[7] = psum.tile([P, CHUNK], F32, tag=work_tags[g % 2], name="out7")
+        for c in range(EARLY_CHUNKS):
+            pending.append((c, g))
+        late.append((6, g))
+        for gg in range(G):
+            late.append((7, gg))
+        emit_passes(len(pending) - pos[0])
+        for c in range(EARLY_CHUNKS):
+            evacuate(c)
+        n6 = 0
+        for c, gg in late[pos[1] :]:
+            if c == 6:
+                n6 += 1
+        emit_passes(n6)
+        evacuate(6)
+        emit_passes(len(late) - pos[1])
+        evacuate(7)

@@ -22,7 +22,6 @@ CHUNK = 512
 LN_EPS = 1e-5
 S_TERMS = 7
 EARLY_CHUNKS = 6
-MX_AFTER = (6, 18, 30)
 V_SPLIT = 24
 
 FLOPS = 2 * 128 * 4096 * 4096
@@ -34,7 +33,7 @@ def tile_tmk_w_kernel(tc, x, design_points, chol_inv_words, chol_inv_scales, out
         ctx.enter_context(tc.manual_schedule())
         const = ctx.enter_context(tc.tile_pool(name="const", bufs=1))
         wpool = ctx.enter_context(tc.tile_pool(name="wpool", bufs=1))
-        terms = ctx.enter_context(tc.tile_pool(name="terms", bufs=16))
+        terms = ctx.enter_context(tc.tile_pool(name="terms", bufs=4))
         chains = ctx.enter_context(tc.tile_pool(name="chains", bufs=2))
         stage = ctx.enter_context(tc.tile_pool(name="stage", bufs=2))
         outp = ctx.enter_context(tc.tile_pool(name="outp", bufs=8))
@@ -128,10 +127,11 @@ def tile_tmk_w_kernel(tc, x, design_points, chol_inv_words, chol_inv_scales, out
         xt = {}
         grouped = {}
         opened = {}
-        t_count = [0]
         pending = []
         late = []
         pos = [0, 0]
+        blocks = {}
+        written = {}
 
         def mx_pass(c, g):
             k4 = 4 * (g % 4)
@@ -156,11 +156,6 @@ def tile_tmk_w_kernel(tc, x, design_points, chol_inv_words, chol_inv_scales, out
                     pos[1] += 1
                     mx_pass(c, g)
 
-        def after_t():
-            t_count[0] += 1
-            if t_count[0] in MX_AFTER:
-                emit_passes(2)
-
         def add_transposed(g, t, src, last):
             nc.tensor.matmul(
                 out=l1[g][:, t * P : (t + 1) * P],
@@ -171,20 +166,25 @@ def tile_tmk_w_kernel(tc, x, design_points, chol_inv_words, chol_inv_scales, out
                 stop=last,
             )
             opened[g] = True
-            after_t()
 
-        def scalar_terms(g, pairs):
-            for t, d in pairs:
-                b = g * T + t
-                term = terms.tile([P, P], F32, tag="term", name="term")
+        def scalar_terms(g, t, dims):
+            b = g * T + t
+            if (g, t) not in blocks:
+                blocks[(g, t)] = terms.tile([P, S_TERMS, P], F32, tag="block", name="block")
+                written[(g, t)] = []
+            for d in dims:
                 nc.scalar.activation(
-                    out=term[:],
+                    out=blocks[(g, t)][:, d, :],
                     in_=xnb[:, d, :],
                     func=ACT.Abs,
                     bias=zh[:, b * D + d : b * D + d + 1],
                     scale=0.5,
                 )
-                add_transposed(g, t, term[:], False)
+                written[(g, t)].append(d)
+
+        def block_in(g, t):
+            for d in reversed(written[(g, t)]):
+                add_transposed(g, t, blocks[(g, t)][:, d, :], False)
 
         def vector_ops(g, lo, hi):
             for i in range(lo, hi):
@@ -192,10 +192,11 @@ def tile_tmk_w_kernel(tc, x, design_points, chol_inv_words, chol_inv_scales, out
                 t = i % T
                 d = v_dims[k]
                 b = g * T + t
+                if i == 0:
+                    sums[g] = chains.tile([P, T, P], F32, tag="sums", name="sums")
                 if k == 0:
-                    sums[(g, t)] = chains.tile([P, P], F32, tag="sum%d" % t, name="sum%d" % t)
                     nc.vector.tensor_scalar(
-                        out=sums[(g, t)][:],
+                        out=sums[g][:, t, :],
                         in0=xnb[:, d, :],
                         scalar1=zf[:, b * D + d : b * D + d + 1],
                         scalar2=kc[:, b : b + 1],
@@ -204,17 +205,17 @@ def tile_tmk_w_kernel(tc, x, design_points, chol_inv_words, chol_inv_scales, out
                     )
                 else:
                     nc.vector.scalar_tensor_tensor(
-                        out=sums[(g, t)][:],
+                        out=sums[g][:, t, :],
                         in0=xnb[:, d, :],
                         scalar=zf[:, b * D + d : b * D + d + 1],
-                        in1=sums[(g, t)][:],
+                        in1=sums[g][:, t, :],
                         op0=ALU.max,
                         op1=ALU.add,
                     )
 
         def vector_sums_in(g):
-            for t in range(T):
-                add_transposed(g, t, sums[(g, t)][:], t == T - 1)
+            for t in reversed(range(T)):
+                add_transposed(g, t, sums[g][:, t, :], t == 0)
 
         def exponent(g):
             kn[g] = stage.tile([P, T * P], BF16, tag="kn", name="kn")
@@ -226,7 +227,6 @@ def tile_tmk_w_kernel(tc, x, design_points, chol_inv_words, chol_inv_scales, out
                 nc.tensor.transpose(
                     out=xt[g][:, t, :], in_=kn[g][:, t * P : (t + 1) * P], identity=ident_b[:]
                 )
-                after_t()
 
         def regroup(g):
             grouped[g] = stage.tile([P, P, T], BF16, tag="grouped", name="grouped", align_bytes=64)
@@ -247,21 +247,29 @@ def tile_tmk_w_kernel(tc, x, design_points, chol_inv_words, chol_inv_scales, out
                 nc.scalar.copy(out=res[:], in_=acc[c][:])
             nc.sync.dma_start(out=out[:, CHUNK * c : CHUNK * (c + 1)], in_=res[:])
 
+        all_s = [d for d in range(S_TERMS)]
         n_vops = T * len(v_dims)
         for g in range(G):
-            t_count[0] = 0
             l1[g] = psum.tile([P, T * P], F32, tag=work_tags[g % 2], name="l1_%d" % g)
             if g == 0:
-                scalar_terms(g, [(t, d) for t in (0, 1) for d in range(4)])
+                scalar_terms(g, 0, all_s[:4])
+                scalar_terms(g, 1, all_s[:4])
                 nc.scalar.copy(out=xnb[:, 4:8, :], in_=spread[1][:])
-                scalar_terms(g, [(t, d) for t in (0, 1) for d in range(4, S_TERMS)])
+                scalar_terms(g, 0, all_s[4:])
+                block_in(g, 0)
+                scalar_terms(g, 1, all_s[4:])
                 vector_ops(g, 0, V_SPLIT)
+                block_in(g, 1)
             else:
+                block_in(g - 1, 3)
                 vector_sums_in(g - 1)
-                scalar_terms(g, [(0, d) for d in range(S_TERMS)])
+                emit_passes(2)
+                scalar_terms(g, 0, all_s)
                 exponent(g - 1)
+                block_in(g, 0)
                 turn_back(g - 1)
-                scalar_terms(g, [(1, d) for d in range(S_TERMS)])
+                emit_passes(2)
+                scalar_terms(g, 1, all_s)
                 regroup(g - 1)
                 if g - 1 == G - 2:
                     acc[6] = psum.tile([P, CHUNK], F32, tag=work_tags[(g - 1) % 2], name="out6")
@@ -269,6 +277,7 @@ def tile_tmk_w_kernel(tc, x, design_points, chol_inv_words, chol_inv_scales, out
                         late.append((6, gg))
                 vector_ops(g, 0, V_SPLIT)
                 quantise(g - 1)
+                block_in(g, 1)
                 if g - 1 == 0:
                     for c in range(EARLY_CHUNKS):
                         acc[c] = psum.tile([P, CHUNK], F32, tag="acc%d" % c, name="out%d" % c)
@@ -276,12 +285,14 @@ def tile_tmk_w_kernel(tc, x, design_points, chol_inv_words, chol_inv_scales, out
                     pending.append((c, g - 1))
                 if g - 1 == G - 2:
                     late.append((6, g - 1))
-            scalar_terms(g, [(2, d) for d in range(S_TERMS)])
-            scalar_terms(g, [(3, d) for d in range(S_TERMS)])
+                emit_passes(2)
+            scalar_terms(g, 2, all_s)
+            block_in(g, 2)
+            scalar_terms(g, 3, all_s)
             vector_ops(g, V_SPLIT, n_vops)
 
         g = G - 1
-        t_count[0] = 100
+        block_in(g, 3)
         vector_sums_in(g)
         emit_passes(3)
         exponent(g)

@@ -22,6 +22,7 @@ CHUNK = 512
 LN_EPS = 1e-5
 S_TERMS = 7
 EARLY_CHUNKS = 6
+MX_AFTER = (6, 18, 30)
 V_SPLIT = 24
 
 FLOPS = 2 * 128 * 4096 * 4096
@@ -33,7 +34,7 @@ def tile_tmk_w_kernel(tc, x, design_points, chol_inv_words, chol_inv_scales, out
         ctx.enter_context(tc.manual_schedule())
         const = ctx.enter_context(tc.tile_pool(name="const", bufs=1))
         wpool = ctx.enter_context(tc.tile_pool(name="wpool", bufs=1))
-        terms = ctx.enter_context(tc.tile_pool(name="terms", bufs=4))
+        terms = ctx.enter_context(tc.tile_pool(name="terms", bufs=16))
         chains = ctx.enter_context(tc.tile_pool(name="chains", bufs=2))
         stage = ctx.enter_context(tc.tile_pool(name="stage", bufs=2))
         outp = ctx.enter_context(tc.tile_pool(name="outp", bufs=8))
@@ -127,11 +128,10 @@ def tile_tmk_w_kernel(tc, x, design_points, chol_inv_words, chol_inv_scales, out
         xt = {}
         grouped = {}
         opened = {}
+        t_count = [0]
         pending = []
         late = []
         pos = [0, 0]
-        blocks = {}
-        written = {}
 
         def mx_pass(c, g):
             k4 = 4 * (g % 4)
@@ -156,6 +156,11 @@ def tile_tmk_w_kernel(tc, x, design_points, chol_inv_words, chol_inv_scales, out
                     pos[1] += 1
                     mx_pass(c, g)
 
+        def after_t():
+            t_count[0] += 1
+            if t_count[0] in MX_AFTER:
+                emit_passes(2)
+
         def add_transposed(g, t, src, last):
             nc.tensor.matmul(
                 out=l1[g][:, t * P : (t + 1) * P],
@@ -166,25 +171,20 @@ def tile_tmk_w_kernel(tc, x, design_points, chol_inv_words, chol_inv_scales, out
                 stop=last,
             )
             opened[g] = True
+            after_t()
 
-        def scalar_terms(g, t, dims):
-            b = g * T + t
-            if (g, t) not in blocks:
-                blocks[(g, t)] = terms.tile([P, S_TERMS, P], F32, tag="block", name="block")
-                written[(g, t)] = []
-            for d in dims:
+        def scalar_terms(g, pairs):
+            for t, d in pairs:
+                b = g * T + t
+                term = terms.tile([P, P], F32, tag="term", name="term")
                 nc.scalar.activation(
-                    out=blocks[(g, t)][:, d, :],
+                    out=term[:],
                     in_=xnb[:, d, :],
                     func=ACT.Abs,
                     bias=zh[:, b * D + d : b * D + d + 1],
                     scale=0.5,
                 )
-                written[(g, t)].append(d)
-
-        def block_in(g, t):
-            for d in reversed(written[(g, t)]):
-                add_transposed(g, t, blocks[(g, t)][:, d, :], False)
+                add_transposed(g, t, term[:], False)
 
         def vector_ops(g, lo, hi):
             for i in range(lo, hi):
@@ -192,11 +192,10 @@ def tile_tmk_w_kernel(tc, x, design_points, chol_inv_words, chol_inv_scales, out
                 t = i % T
                 d = v_dims[k]
                 b = g * T + t
-                if i == 0:
-                    sums[g] = chains.tile([P, T, P], F32, tag="sums", name="sums")
                 if k == 0:
+                    sums[(g, t)] = chains.tile([P, P], F32, tag="sum%d" % t, name="sum%d" % t)
                     nc.vector.tensor_scalar(
-                        out=sums[g][:, t, :],
+                        out=sums[(g, t)][:],
                         in0=xnb[:, d, :],
                         scalar1=zf[:, b * D + d : b * D + d + 1],
                         scalar2=kc[:, b : b + 1],
@@ -205,17 +204,17 @@ def tile_tmk_w_kernel(tc, x, design_points, chol_inv_words, chol_inv_scales, out
                     )
                 else:
                     nc.vector.scalar_tensor_tensor(
-                        out=sums[g][:, t, :],
+                        out=sums[(g, t)][:],
                         in0=xnb[:, d, :],
                         scalar=zf[:, b * D + d : b * D + d + 1],
-                        in1=sums[g][:, t, :],
+                        in1=sums[(g, t)][:],
                         op0=ALU.max,
                         op1=ALU.add,
                     )
 
         def vector_sums_in(g):
-            for t in reversed(range(T)):
-                add_transposed(g, t, sums[g][:, t, :], t == 0)
+            for t in range(T):
+                add_transposed(g, t, sums[(g, t)][:], t == T - 1)
 
         def exponent(g):
             kn[g] = stage.tile([P, T * P], BF16, tag="kn", name="kn")
@@ -227,6 +226,7 @@ def tile_tmk_w_kernel(tc, x, design_points, chol_inv_words, chol_inv_scales, out
                 nc.tensor.transpose(
                     out=xt[g][:, t, :], in_=kn[g][:, t * P : (t + 1) * P], identity=ident_b[:]
                 )
+                after_t()
 
         def regroup(g):
             grouped[g] = stage.tile([P, P, T], BF16, tag="grouped", name="grouped", align_bytes=64)
@@ -247,29 +247,22 @@ def tile_tmk_w_kernel(tc, x, design_points, chol_inv_words, chol_inv_scales, out
                 nc.scalar.copy(out=res[:], in_=acc[c][:])
             nc.sync.dma_start(out=out[:, CHUNK * c : CHUNK * (c + 1)], in_=res[:])
 
-        all_s = [d for d in range(S_TERMS)]
         n_vops = T * len(v_dims)
+        order = [(t, d) for d in range(S_TERMS) for t in range(T)]
         for g in range(G):
+            t_count[0] = 0
             l1[g] = psum.tile([P, T * P], F32, tag=work_tags[g % 2], name="l1_%d" % g)
             if g == 0:
-                scalar_terms(g, 0, all_s[:4])
-                scalar_terms(g, 1, all_s[:4])
+                scalar_terms(g, order[0:16])
                 nc.scalar.copy(out=xnb[:, 4:8, :], in_=spread[1][:])
-                scalar_terms(g, 0, all_s[4:])
-                block_in(g, 0)
-                scalar_terms(g, 1, all_s[4:])
                 vector_ops(g, 0, V_SPLIT)
-                block_in(g, 1)
+                scalar_terms(g, order[16:28])
             else:
-                block_in(g - 1, 3)
                 vector_sums_in(g - 1)
-                emit_passes(2)
-                scalar_terms(g, 0, all_s)
+                scalar_terms(g, order[0:7])
                 exponent(g - 1)
-                block_in(g, 0)
                 turn_back(g - 1)
-                emit_passes(2)
-                scalar_terms(g, 1, all_s)
+                scalar_terms(g, order[7:14])
                 regroup(g - 1)
                 if g - 1 == G - 2:
                     acc[6] = psum.tile([P, CHUNK], F32, tag=work_tags[(g - 1) % 2], name="out6")
@@ -277,7 +270,6 @@ def tile_tmk_w_kernel(tc, x, design_points, chol_inv_words, chol_inv_scales, out
                         late.append((6, gg))
                 vector_ops(g, 0, V_SPLIT)
                 quantise(g - 1)
-                block_in(g, 1)
                 if g - 1 == 0:
                     for c in range(EARLY_CHUNKS):
                         acc[c] = psum.tile([P, CHUNK], F32, tag="acc%d" % c, name="out%d" % c)
@@ -285,14 +277,11 @@ def tile_tmk_w_kernel(tc, x, design_points, chol_inv_words, chol_inv_scales, out
                     pending.append((c, g - 1))
                 if g - 1 == G - 2:
                     late.append((6, g - 1))
-                emit_passes(2)
-            scalar_terms(g, 2, all_s)
-            block_in(g, 2)
-            scalar_terms(g, 3, all_s)
+                scalar_terms(g, order[14:28])
             vector_ops(g, V_SPLIT, n_vops)
 
         g = G - 1
-        block_in(g, 3)
+        t_count[0] = 100
         vector_sums_in(g)
         emit_passes(3)
         exponent(g)

@@ -20,10 +20,12 @@ T = 4
 COLS = 4096
 CHUNK = 512
 LN_EPS = 1e-5
-S_TERMS = 7
+S_TERMS = 6
 EARLY_CHUNKS = 6
-MX_AFTER = (6, 18, 30)
+MX_AFTER = (6, 16, 27)
+MX_AFTER_FIRST = (4, 12, 20)
 V_SPLIT = 24
+PREWARM = 6
 
 FLOPS = 2 * 128 * 4096 * 4096
 
@@ -65,6 +67,8 @@ def tile_tmk_w_kernel(tc, x, design_points, chol_inv_words, chol_inv_scales, out
             )
             w_words.append(wt)
 
+        warm_src = const.tile([P, CHUNK], BF16, name="warm_src")
+        nc.gpsimd.memset(warm_src[:], 0.0)
         neg_half = const.tile([P, 1], F32, name="neg_half")
         nc.gpsimd.memset(neg_half[:], -0.5)
         scratch = const.tile([P, 1], F32, name="scratch")
@@ -92,8 +96,17 @@ def tile_tmk_w_kernel(tc, x, design_points, chol_inv_words, chol_inv_scales, out
         )
 
         xnb = const.tile([P, D, P], F32, name="xnb")
+        warm = psum.tile([P, CHUNK], F32, tag="acc5", name="warm")
+
+        def idle_matmuls(n):
+            for i in range(n):
+                nc.tensor.matmul(out=warm[:], lhsT=warm_src[:, 0:P], rhs=warm_src[:], start=True, stop=True)
+
+        idle_matmuls(PREWARM)
         spread = {}
         for k in (0, 2, 1, 3):
+            if k == 1:
+                idle_matmuls(2)
             spread[k] = psum.tile([P, 4, P], F32, tag="acc%d" % k, name="bc%d" % k)
             for j in range(4):
                 d = 4 * k + j
@@ -129,6 +142,7 @@ def tile_tmk_w_kernel(tc, x, design_points, chol_inv_words, chol_inv_scales, out
         grouped = {}
         opened = {}
         t_count = [0]
+        points = [MX_AFTER_FIRST]
         pending = []
         late = []
         pos = [0, 0]
@@ -155,10 +169,12 @@ def tile_tmk_w_kernel(tc, x, design_points, chol_inv_words, chol_inv_scales, out
                     c, g = late[pos[1]]
                     pos[1] += 1
                     mx_pass(c, g)
+                elif len(pending) == 0:
+                    idle_matmuls(1)
 
         def after_t():
             t_count[0] += 1
-            if t_count[0] in MX_AFTER:
+            if t_count[0] in points[0]:
                 emit_passes(2)
 
         def add_transposed(g, t, src, last):
@@ -251,18 +267,19 @@ def tile_tmk_w_kernel(tc, x, design_points, chol_inv_words, chol_inv_scales, out
         order = [(t, d) for d in range(S_TERMS) for t in range(T)]
         for g in range(G):
             t_count[0] = 0
+            points[0] = MX_AFTER if g > 0 else MX_AFTER_FIRST
             l1[g] = psum.tile([P, T * P], F32, tag=work_tags[g % 2], name="l1_%d" % g)
             if g == 0:
                 scalar_terms(g, order[0:16])
                 nc.scalar.copy(out=xnb[:, 4:8, :], in_=spread[1][:])
                 vector_ops(g, 0, V_SPLIT)
-                scalar_terms(g, order[16:28])
+                scalar_terms(g, order[16 : T * S_TERMS])
             else:
                 vector_sums_in(g - 1)
-                scalar_terms(g, order[0:7])
+                scalar_terms(g, order[0:S_TERMS])
                 exponent(g - 1)
                 turn_back(g - 1)
-                scalar_terms(g, order[7:14])
+                scalar_terms(g, order[S_TERMS : 2 * S_TERMS])
                 regroup(g - 1)
                 if g - 1 == G - 2:
                     acc[6] = psum.tile([P, CHUNK], F32, tag=work_tags[(g - 1) % 2], name="out6")
@@ -277,7 +294,7 @@ def tile_tmk_w_kernel(tc, x, design_points, chol_inv_words, chol_inv_scales, out
                     pending.append((c, g - 1))
                 if g - 1 == G - 2:
                     late.append((6, g - 1))
-                scalar_terms(g, order[14:28])
+                scalar_terms(g, order[2 * S_TERMS : T * S_TERMS])
             vector_ops(g, V_SPLIT, n_vops)
 
         g = G - 1

@@ -20,11 +20,14 @@ T = 4
 COLS = 4096
 CHUNK = 512
 LN_EPS = 1e-5
-S_TERMS = 6
+S_OF_BLOCK = (7, 7, 6, 6)
+CUT_E = 8
+CUT_C = 16
+EXP_PARTS = ((0, 2), (2, 4))
 EARLY_CHUNKS = 6
-MX_AFTER = (6, 16, 27)
+MX_AFTER = (6, 17, 29)
 MX_AFTER_FIRST = (4, 12, 20)
-V_SPLIT = 24
+V_SPLIT = 28
 PREWARM = 6
 
 FLOPS = 2 * 128 * 4096 * 4096
@@ -116,15 +119,18 @@ def tile_tmk_w_kernel(tc, x, design_points, chol_inv_words, chol_inv_scales, out
 
         zh = const.tile([P, G * T * D], F32, name="zh")
         nc.vector.tensor_scalar_mul(out=zh[:], in0=zf[:], scalar1=-0.5)
-        kc = const.tile([P, G * T], F32, name="kc")
-        nc.vector.tensor_reduce(
-            out=kc[:],
-            in_=zh[:].rearrange("p (b d) -> p b d", d=D)[:, :, S_TERMS:D],
-            axis=AX.X,
-            op=ALU.add,
-        )
-        exp_bias = const.tile([P, 1], F32, name="exp_bias")
-        nc.vector.tensor_reduce(out=exp_bias[:], in_=xn[:, S_TERMS:D], axis=AX.X, op=ALU.add)
+        kc = {}
+        exp_bias = {}
+        for s in sorted(set(S_OF_BLOCK)):
+            kc[s] = const.tile([P, G * T], F32, name="kc%d" % s)
+            nc.vector.tensor_reduce(
+                out=kc[s][:],
+                in_=zh[:].rearrange("p (b d) -> p b d", d=D)[:, :, s:D],
+                axis=AX.X,
+                op=ALU.add,
+            )
+            exp_bias[s] = const.tile([P, 1], F32, name="exp_bias%d" % s)
+            nc.vector.tensor_reduce(out=exp_bias[s][:], in_=xn[:, s:D], axis=AX.X, op=ALU.add)
         nc.scalar.copy(out=xnb[:, 0:4, :], in_=spread[0][:])
         nc.vector.tensor_copy(out=xnb[:, 8:12, :], in_=spread[2][:])
         nc.vector.tensor_copy(out=xnb[:, 12:16, :], in_=spread[3][:])
@@ -133,7 +139,8 @@ def tile_tmk_w_kernel(tc, x, design_points, chol_inv_words, chol_inv_scales, out
         kscales = const.tile([P, G, P], U8, name="kscales", align_bytes=64)
 
         work_tags = ("wka", "wkb")
-        v_dims = [d for d in range(8, D)] + [d for d in range(S_TERMS, 8)]
+        v_dims = [[d for d in range(8, D)] + [d for d in range(s, 8)] for s in S_OF_BLOCK]
+        v_list = [(k, t) for k in range(D) for t in range(T) if k < len(v_dims[t])]
         acc = {}
         l1 = {}
         sums = {}
@@ -203,10 +210,8 @@ def tile_tmk_w_kernel(tc, x, design_points, chol_inv_words, chol_inv_scales, out
                 add_transposed(g, t, term[:], False)
 
         def vector_ops(g, lo, hi):
-            for i in range(lo, hi):
-                k = i // T
-                t = i % T
-                d = v_dims[k]
+            for k, t in v_list[lo:hi]:
+                d = v_dims[t][k]
                 b = g * T + t
                 if k == 0:
                     sums[(g, t)] = chains.tile([P, P], F32, tag="sum%d" % t, name="sum%d" % t)
@@ -214,7 +219,7 @@ def tile_tmk_w_kernel(tc, x, design_points, chol_inv_words, chol_inv_scales, out
                         out=sums[(g, t)][:],
                         in0=xnb[:, d, :],
                         scalar1=zf[:, b * D + d : b * D + d + 1],
-                        scalar2=kc[:, b : b + 1],
+                        scalar2=kc[S_OF_BLOCK[t]][:, b : b + 1],
                         op0=ALU.max,
                         op1=ALU.add,
                     )
@@ -234,7 +239,14 @@ def tile_tmk_w_kernel(tc, x, design_points, chol_inv_words, chol_inv_scales, out
 
         def exponent(g):
             kn[g] = stage.tile([P, T * P], BF16, tag="kn", name="kn")
-            nc.scalar.activation(out=kn[g][:], in_=l1[g][:], func=ACT.Exp, bias=exp_bias[:], scale=-2.0)
+            for lo, hi in EXP_PARTS:
+                nc.scalar.activation(
+                    out=kn[g][:, lo * P : hi * P],
+                    in_=l1[g][:, lo * P : hi * P],
+                    func=ACT.Exp,
+                    bias=exp_bias[S_OF_BLOCK[lo]][:],
+                    scale=-2.0,
+                )
 
         def turn_back(g):
             xt[g] = psum.tile([P, T, P], BF16, tag=work_tags[g % 2], name="xt_%d" % g)
@@ -263,8 +275,8 @@ def tile_tmk_w_kernel(tc, x, design_points, chol_inv_words, chol_inv_scales, out
                 nc.scalar.copy(out=res[:], in_=acc[c][:])
             nc.sync.dma_start(out=out[:, CHUNK * c : CHUNK * (c + 1)], in_=res[:])
 
-        n_vops = T * len(v_dims)
-        order = [(t, d) for d in range(S_TERMS) for t in range(T)]
+        n_vops = len(v_list)
+        order = [(t, d) for d in range(D) for t in range(T) if d < S_OF_BLOCK[t]]
         for g in range(G):
             t_count[0] = 0
             points[0] = MX_AFTER if g > 0 else MX_AFTER_FIRST
@@ -273,13 +285,13 @@ def tile_tmk_w_kernel(tc, x, design_points, chol_inv_words, chol_inv_scales, out
                 scalar_terms(g, order[0:16])
                 nc.scalar.copy(out=xnb[:, 4:8, :], in_=spread[1][:])
                 vector_ops(g, 0, V_SPLIT)
-                scalar_terms(g, order[16 : T * S_TERMS])
+                scalar_terms(g, order[16:])
             else:
                 vector_sums_in(g - 1)
-                scalar_terms(g, order[0:S_TERMS])
+                scalar_terms(g, order[0:CUT_E])
                 exponent(g - 1)
                 turn_back(g - 1)
-                scalar_terms(g, order[S_TERMS : 2 * S_TERMS])
+                scalar_terms(g, order[CUT_E:CUT_C])
                 regroup(g - 1)
                 if g - 1 == G - 2:
                     acc[6] = psum.tile([P, CHUNK], F32, tag=work_tags[(g - 1) % 2], name="out6")
@@ -294,16 +306,16 @@ def tile_tmk_w_kernel(tc, x, design_points, chol_inv_words, chol_inv_scales, out
                     pending.append((c, g - 1))
                 if g - 1 == G - 2:
                     late.append((6, g - 1))
-                scalar_terms(g, order[2 * S_TERMS : T * S_TERMS])
+                scalar_terms(g, order[CUT_C:])
             vector_ops(g, V_SPLIT, n_vops)
 
         g = G - 1
         t_count[0] = 100
         vector_sums_in(g)
-        emit_passes(3)
+        emit_passes(4)
         exponent(g)
         turn_back(g)
-        emit_passes(4)
+        emit_passes(6)
         regroup(g)
         quantise(g)
         acc[7] = psum.tile([P, CHUNK], F32, tag=work_tags[g % 2], name="out7")

@@ -20,12 +20,10 @@ T = 4
 COLS = 4096
 CHUNK = 512
 LN_EPS = 1e-5
-S_OF_BLOCK = (7, 7, 6, 6)
+S_OF_ROUND = (7, 6, 7, 6, 7, 6, 7, 6)
 CUT_E = 8
 CUT_C = 16
-EXP_PARTS = ((0, 2), (2, 4))
 EARLY_CHUNKS = 6
-MX_AFTER = (6, 17, 29)
 MX_AFTER_FIRST = (4, 12, 20)
 V_SPLIT = 28
 PREWARM = 6
@@ -80,8 +78,6 @@ def tile_tmk_w_kernel(tc, x, design_points, chol_inv_words, chol_inv_scales, out
         nc.scalar.activation(out=scratch2[:], in_=scratch[:], func=ACT.Exp)
         ident_f = const.tile([P, P], F32, name="ident_f")
         make_identity(nc, ident_f[:])
-        ident_b = const.tile([P, P], BF16, name="ident_b")
-        make_identity(nc, ident_b[:])
 
         stats = const.tile([P, 6], F32, name="stats")
         nc.vector.bn_stats(out=stats[:], in_=x_sb[:])
@@ -121,7 +117,7 @@ def tile_tmk_w_kernel(tc, x, design_points, chol_inv_words, chol_inv_scales, out
         nc.vector.tensor_scalar_mul(out=zh[:], in0=zf[:], scalar1=-0.5)
         kc = {}
         exp_bias = {}
-        for s in sorted(set(S_OF_BLOCK)):
+        for s in sorted(set(S_OF_ROUND)):
             kc[s] = const.tile([P, G * T], F32, name="kc%d" % s)
             nc.vector.tensor_reduce(
                 out=kc[s][:],
@@ -139,8 +135,7 @@ def tile_tmk_w_kernel(tc, x, design_points, chol_inv_words, chol_inv_scales, out
         kscales = const.tile([P, G, P], U8, name="kscales", align_bytes=64)
 
         work_tags = ("wka", "wkb")
-        v_dims = [[d for d in range(8, D)] + [d for d in range(s, 8)] for s in S_OF_BLOCK]
-        v_list = [(k, t) for k in range(D) for t in range(T) if k < len(v_dims[t])]
+        v_dims = [[d for d in range(8, D)] + [d for d in range(s, 8)] for s in S_OF_ROUND]
         acc = {}
         l1 = {}
         sums = {}
@@ -210,8 +205,8 @@ def tile_tmk_w_kernel(tc, x, design_points, chol_inv_words, chol_inv_scales, out
                 add_transposed(g, t, term[:], False)
 
         def vector_ops(g, lo, hi):
-            for k, t in v_list[lo:hi]:
-                d = v_dims[t][k]
+            for k, t in [(k, t) for k in range(len(v_dims[g])) for t in range(T)][lo:hi]:
+                d = v_dims[g][k]
                 b = g * T + t
                 if k == 0:
                     sums[(g, t)] = chains.tile([P, P], F32, tag="sum%d" % t, name="sum%d" % t)
@@ -219,7 +214,7 @@ def tile_tmk_w_kernel(tc, x, design_points, chol_inv_words, chol_inv_scales, out
                         out=sums[(g, t)][:],
                         in0=xnb[:, d, :],
                         scalar1=zf[:, b * D + d : b * D + d + 1],
-                        scalar2=kc[S_OF_BLOCK[t]][:, b : b + 1],
+                        scalar2=kc[S_OF_ROUND[g]][:, b : b + 1],
                         op0=ALU.max,
                         op1=ALU.add,
                     )
@@ -238,27 +233,28 @@ def tile_tmk_w_kernel(tc, x, design_points, chol_inv_words, chol_inv_scales, out
                 add_transposed(g, t, sums[(g, t)][:], t == T - 1)
 
         def exponent(g):
-            kn[g] = stage.tile([P, T * P], BF16, tag="kn", name="kn")
-            for lo, hi in EXP_PARTS:
-                nc.scalar.activation(
-                    out=kn[g][:, lo * P : hi * P],
-                    in_=l1[g][:, lo * P : hi * P],
-                    func=ACT.Exp,
-                    bias=exp_bias[S_OF_BLOCK[lo]][:],
-                    scale=-2.0,
-                )
+            kn[g] = stage.tile([P, P, T], BF16, tag="kn", name="kn")
+            nc.scalar.activation(
+                out=kn[g][:],
+                in_=l1[g][:].rearrange("n (t p) -> n p t", t=T),
+                func=ACT.Exp,
+                bias=exp_bias[S_OF_ROUND[g]][:],
+                scale=-2.0,
+            )
 
         def turn_back(g):
-            xt[g] = psum.tile([P, T, P], BF16, tag=work_tags[g % 2], name="xt_%d" % g)
-            for t in range(T):
-                nc.tensor.transpose(
-                    out=xt[g][:, t, :], in_=kn[g][:, t * P : (t + 1) * P], identity=ident_b[:]
-                )
+            xt[g] = psum.tile([P, 2, P], F32, tag=work_tags[g % 2], name="xt_%d" % g)
+            words = kn[g][:].rearrange("n p t -> n (p t)").bitcast(F32)
+            for u in range(2):
+                nc.tensor.transpose(out=xt[g][:, u, :], in_=words[:, u : 2 * P : 2], identity=ident_f[:])
                 after_t()
 
         def regroup(g):
             grouped[g] = stage.tile([P, P, T], BF16, tag="grouped", name="grouped", align_bytes=64)
-            nc.scalar.copy(out=grouped[g][:], in_=xt[g][:].rearrange("p t n -> p n t"))
+            nc.scalar.copy(
+                out=grouped[g][:].rearrange("p n t -> p (n t)").bitcast(F32).rearrange("p (n u) -> p n u", u=2),
+                in_=xt[g][:].rearrange("p u n -> p n u"),
+            )
 
         def quantise(g):
             nc.vector.quantize_mx(
@@ -275,11 +271,12 @@ def tile_tmk_w_kernel(tc, x, design_points, chol_inv_words, chol_inv_scales, out
                 nc.scalar.copy(out=res[:], in_=acc[c][:])
             nc.sync.dma_start(out=out[:, CHUNK * c : CHUNK * (c + 1)], in_=res[:])
 
-        n_vops = len(v_list)
-        order = [(t, d) for d in range(D) for t in range(T) if d < S_OF_BLOCK[t]]
         for g in range(G):
+            n_vops = T * len(v_dims[g])
+            order = [(t, d) for d in range(S_OF_ROUND[g]) for t in range(T)]
+            n_turns = T + len(order) + 2
             t_count[0] = 0
-            points[0] = MX_AFTER if g > 0 else MX_AFTER_FIRST
+            points[0] = tuple(6 + (n_turns * i) // 3 for i in range(3)) if g > 0 else MX_AFTER_FIRST
             l1[g] = psum.tile([P, T * P], F32, tag=work_tags[g % 2], name="l1_%d" % g)
             if g == 0:
                 scalar_terms(g, order[0:16])

@@ -20,7 +20,7 @@ T = 4
 COLS = 4096
 CHUNK = 512
 LN_EPS = 1e-5
-S_OF_ROUND = (7, 6, 7, 6, 7, 6, 7, 6)
+S_OF_ROUND = (8, 6, 7, 6, 7, 6, 7, 6)
 CUT_E = 8
 CUT_C = 16
 EARLY_CHUNKS = 6
@@ -76,6 +76,10 @@ def tile_tmk_w_kernel(tc, x, design_points, chol_inv_words, chol_inv_scales, out
         nc.gpsimd.memset(scratch[:], 0.0)
         scratch2 = const.tile([P, 1], F32, name="scratch2")
         nc.scalar.activation(out=scratch2[:], in_=scratch[:], func=ACT.Exp)
+        zh = const.tile([P, G * T * D], F32, name="zh")
+        nc.scalar.activation(out=zh[:], in_=z_sb[:].rearrange("p g k -> p (g k)"), func=ACT.Copy, scale=-0.5)
+        zf = const.tile([P, G * T * D], F32, name="zf")
+        nc.scalar.copy(out=zf[:], in_=z_sb[:].rearrange("p g k -> p (g k)"))
         ident_f = const.tile([P, P], F32, name="ident_f")
         make_identity(nc, ident_f[:])
 
@@ -87,8 +91,6 @@ def tile_tmk_w_kernel(tc, x, design_points, chol_inv_words, chol_inv_scales, out
         nc.vector.tensor_scalar_add(out=vare[:], in0=mv[:, 1:2], scalar1=LN_EPS)
         rstd = const.tile([P, 1], F32, name="rstd")
         nc.gpsimd.tensor_tensor(out=rstd[:], in0=vare[:], in1=neg_half[:], op=ALU.pow)
-        zf = const.tile([P, G * T * D], F32, name="zf")
-        nc.vector.tensor_copy(out=zf[:], in_=z_sb[:].rearrange("p g k -> p (g k)"))
         xn = const.tile([P, D], F32, name="xn")
         nc.vector.tensor_scalar(
             out=xn[:], in0=x_sb[:], scalar1=mv[:, 0:1], scalar2=rstd[:], op0=ALU.subtract, op1=ALU.mult
@@ -113,23 +115,29 @@ def tile_tmk_w_kernel(tc, x, design_points, chol_inv_words, chol_inv_scales, out
                     out=spread[k][:, j, :], in_=xn[:, d : d + 1].to_broadcast([P, P]), identity=ident_f[:]
                 )
 
-        zh = const.tile([P, G * T * D], F32, name="zh")
-        nc.vector.tensor_scalar_mul(out=zh[:], in0=zf[:], scalar1=-0.5)
-        kc = {}
+        kc = const.tile([P, G * T], F32, name="kc")
         exp_bias = {}
-        for s in sorted(set(S_OF_ROUND)):
-            kc[s] = const.tile([P, G * T], F32, name="kc%d" % s)
+        nc.vector.tensor_reduce(
+            out=kc[:, 0:T],
+            in_=zh[:, 0 : T * D].rearrange("p (b d) -> p b d", d=D)[:, :, S_OF_ROUND[0] : D],
+            axis=AX.X,
+            op=ALU.add,
+        )
+        for first in (1, 2):
+            s = S_OF_ROUND[first]
             nc.vector.tensor_reduce(
-                out=kc[s][:],
-                in_=zh[:].rearrange("p (b d) -> p b d", d=D)[:, :, s:D],
+                out=kc[:].rearrange("p (h two b) -> p h two b", two=2, b=T)[:, first // 2 : G // 2, first % 2, :],
+                in_=zh[:].rearrange("p (h two b d) -> p h two b d", two=2, b=T, d=D)[
+                    :, first // 2 : G // 2, first % 2, :, s:D
+                ],
                 axis=AX.X,
                 op=ALU.add,
             )
+        for s in sorted(set(S_OF_ROUND)):
             exp_bias[s] = const.tile([P, 1], F32, name="exp_bias%d" % s)
             nc.vector.tensor_reduce(out=exp_bias[s][:], in_=xn[:, s:D], axis=AX.X, op=ALU.add)
         nc.scalar.copy(out=xnb[:, 0:4, :], in_=spread[0][:])
         nc.vector.tensor_copy(out=xnb[:, 8:12, :], in_=spread[2][:])
-        nc.vector.tensor_copy(out=xnb[:, 12:16, :], in_=spread[3][:])
 
         kcodes = const.tile([P, G, P], U32, name="kcodes", align_bytes=64)
         kscales = const.tile([P, G, P], U8, name="kscales", align_bytes=64)
@@ -214,7 +222,7 @@ def tile_tmk_w_kernel(tc, x, design_points, chol_inv_words, chol_inv_scales, out
                         out=sums[(g, t)][:],
                         in0=xnb[:, d, :],
                         scalar1=zf[:, b * D + d : b * D + d + 1],
-                        scalar2=kc[S_OF_ROUND[g]][:, b : b + 1],
+                        scalar2=kc[:, b : b + 1],
                         op0=ALU.max,
                         op1=ALU.add,
                     )
@@ -281,7 +289,9 @@ def tile_tmk_w_kernel(tc, x, design_points, chol_inv_words, chol_inv_scales, out
             if g == 0:
                 scalar_terms(g, order[0:16])
                 nc.scalar.copy(out=xnb[:, 4:8, :], in_=spread[1][:])
-                vector_ops(g, 0, V_SPLIT)
+                vector_ops(g, 0, 16)
+                nc.vector.tensor_copy(out=xnb[:, 12:16, :], in_=spread[3][:])
+                vector_ops(g, 16, V_SPLIT)
                 scalar_terms(g, order[16:])
             else:
                 vector_sums_in(g - 1)

@@ -241,10 +241,10 @@ def tile_tmk_w_kernel(tc, x, design_points, chol_inv_words, chol_inv_scales, out
                 add_transposed(g, t, sums[(g, t)][:], t == T - 1)
 
         def exponent(g):
-            kn[g] = stage.tile([P, P, T], BF16, tag="kn", name="kn")
+            kn[g] = stage.tile([P, 2, P, 2], BF16, tag="kn", name="kn")
             nc.scalar.activation(
                 out=kn[g][:],
-                in_=l1[g][:].rearrange("n (t p) -> n p t", t=T),
+                in_=l1[g][:].rearrange("n (u e p) -> n u p e", u=2, e=2),
                 func=ACT.Exp,
                 bias=exp_bias[S_OF_ROUND[g]][:],
                 scale=-2.0,
@@ -252,9 +252,9 @@ def tile_tmk_w_kernel(tc, x, design_points, chol_inv_words, chol_inv_scales, out
 
         def turn_back(g):
             xt[g] = psum.tile([P, 2, P], F32, tag=work_tags[g % 2], name="xt_%d" % g)
-            words = kn[g][:].rearrange("n p t -> n (p t)").bitcast(F32)
+            words = kn[g][:].rearrange("n u p e -> n (u p e)").bitcast(F32)
             for u in range(2):
-                nc.tensor.transpose(out=xt[g][:, u, :], in_=words[:, u : 2 * P : 2], identity=ident_f[:])
+                nc.tensor.transpose(out=xt[g][:, u, :], in_=words[:, u * P : (u + 1) * P], identity=ident_f[:])
                 after_t()
 
         def regroup(g):
@@ -325,20 +325,31 @@ def tile_tmk_w_kernel(tc, x, design_points, chol_inv_words, chol_inv_scales, out
         emit_passes(6)
         regroup(g)
         quantise(g)
-        acc[7] = psum.tile([P, CHUNK], F32, tag=work_tags[g % 2], name="out7")
         for c in range(EARLY_CHUNKS):
             pending.append((c, g))
         late.append((6, g))
-        for gg in range(G):
-            late.append((7, gg))
         emit_passes(len(pending) - pos[0])
         for c in range(EARLY_CHUNKS):
             evacuate(c)
-        n6 = 0
-        for c, gg in late[pos[1] :]:
-            if c == 6:
-                n6 += 1
-        emit_passes(n6)
-        evacuate(6)
         emit_passes(len(late) - pos[1])
-        evacuate(7)
+        evacuate(6)
+        half = CHUNK // 2
+        for h, tag in enumerate((work_tags[g % 2], "acc0")):
+            part = psum.tile([P, half], F32, tag=tag, name="out7_%d" % h)
+            lo = CHUNK * 7 + half * h
+            for gg in range(G):
+                nc.tensor.matmul_mx(
+                    out=part[:],
+                    lhsT=kcodes[:, gg, :].bitcast(FP8X4),
+                    lhsT_scale=kscales[:, gg, :],
+                    rhs=w_words[gg][:, 4 * lo : 4 * (lo + half)].bitcast(FP8X4),
+                    rhs_scale=w_scales[4 * (gg % 4) : P, gg // 4, lo : lo + half],
+                    start=(gg == 0),
+                    stop=(gg == G - 1),
+                )
+            res = outp.tile([P, half], F32, tag="res", name="res7_%d" % h)
+            if h == 0:
+                nc.vector.tensor_copy(out=res[:], in_=part[:])
+            else:
+                nc.scalar.copy(out=res[:], in_=part[:])
+            nc.sync.dma_start(out=out[:, lo : lo + half], in_=res[:])

@@ -275,9 +275,10 @@ def tile_tmk_w_kernel(tc, x, design_points, chol_inv_words, chol_inv_scales, out
             res = outp.tile([P, CHUNK], F32, tag="res", name="res%d" % c)
             if c % 2 == 0:
                 nc.vector.tensor_copy(out=res[:], in_=acc[c][:])
+                nc.sync.dma_start(out=out[:, CHUNK * c : CHUNK * (c + 1)], in_=res[:])
             else:
                 nc.scalar.copy(out=res[:], in_=acc[c][:])
-            nc.sync.dma_start(out=out[:, CHUNK * c : CHUNK * (c + 1)], in_=res[:])
+                nc.scalar.dma_start(out=out[:, CHUNK * c : CHUNK * (c + 1)], in_=res[:])
 
         for g in range(G):
             n_vops = T * len(v_dims[g])
@@ -350,6 +351,7 @@ def tile_tmk_w_kernel(tc, x, design_points, chol_inv_words, chol_inv_scales, out
             res = outp.tile([P, half], F32, tag="res", name="res7_%d" % h)
             if h == 0:
                 nc.vector.tensor_copy(out=res[:], in_=part[:])
+                nc.sync.dma_start(out=out[:, lo : lo + half], in_=res[:])
             else:
                 nc.scalar.copy(out=res[:], in_=part[:])
-            nc.sync.dma_start(out=out[:, lo : lo + half], in_=res[:])
+                nc.scalar.dma_start(out=out[:, lo : lo + half], in_=res[:])

@@ -20,7 +20,7 @@ T = 4
 COLS = 4096
 CHUNK = 512
 LN_EPS = 1e-5
-S_OF_ROUND = (8, 6, 7, 6, 7, 6, 7, 6)
+S_OF_ROUND = (8, 7, 7, 6, 7, 6, 7, 6)
 CUT_E = 8
 CUT_C = 16
 EARLY_CHUNKS = 6
@@ -117,13 +117,14 @@ def tile_tmk_w_kernel(tc, x, design_points, chol_inv_words, chol_inv_scales, out
 
         kc = const.tile([P, G * T], F32, name="kc")
         exp_bias = {}
-        nc.vector.tensor_reduce(
-            out=kc[:, 0:T],
-            in_=zh[:, 0 : T * D].rearrange("p (b d) -> p b d", d=D)[:, :, S_OF_ROUND[0] : D],
-            axis=AX.X,
-            op=ALU.add,
-        )
-        for first in (1, 2):
+        for g in (0, 1):
+            nc.vector.tensor_reduce(
+                out=kc[:, g * T : (g + 1) * T],
+                in_=zh[:, g * T * D : (g + 1) * T * D].rearrange("p (b d) -> p b d", d=D)[:, :, S_OF_ROUND[g] : D],
+                axis=AX.X,
+                op=ALU.add,
+            )
+        for first in (2, 3):
             s = S_OF_ROUND[first]
             nc.vector.tensor_reduce(
                 out=kc[:].rearrange("p (h two b) -> p h two b", two=2, b=T)[:, first // 2 : G // 2, first % 2, :],

@@ -76,10 +76,6 @@ def tile_tmk_w_kernel(tc, x, design_points, chol_inv_words, chol_inv_scales, out
         nc.gpsimd.memset(scratch[:], 0.0)
         scratch2 = const.tile([P, 1], F32, name="scratch2")
         nc.scalar.activation(out=scratch2[:], in_=scratch[:], func=ACT.Exp)
-        zh = const.tile([P, G * T * D], F32, name="zh")
-        nc.scalar.activation(out=zh[:], in_=z_sb[:].rearrange("p g k -> p (g k)"), func=ACT.Copy, scale=-0.5)
-        zf = const.tile([P, G * T * D], F32, name="zf")
-        nc.scalar.copy(out=zf[:], in_=z_sb[:].rearrange("p g k -> p (g k)"))
         ident_f = const.tile([P, P], F32, name="ident_f")
         make_identity(nc, ident_f[:])
 
@@ -91,6 +87,8 @@ def tile_tmk_w_kernel(tc, x, design_points, chol_inv_words, chol_inv_scales, out
         nc.vector.tensor_scalar_add(out=vare[:], in0=mv[:, 1:2], scalar1=LN_EPS)
         rstd = const.tile([P, 1], F32, name="rstd")
         nc.gpsimd.tensor_tensor(out=rstd[:], in0=vare[:], in1=neg_half[:], op=ALU.pow)
+        zf = const.tile([P, G * T * D], F32, name="zf")
+        nc.vector.tensor_copy(out=zf[:], in_=z_sb[:].rearrange("p g k -> p (g k)"))
         xn = const.tile([P, D], F32, name="xn")
         nc.vector.tensor_scalar(
             out=xn[:], in0=x_sb[:], scalar1=mv[:, 0:1], scalar2=rstd[:], op0=ALU.subtract, op1=ALU.mult
@@ -115,6 +113,8 @@ def tile_tmk_w_kernel(tc, x, design_points, chol_inv_words, chol_inv_scales, out
                     out=spread[k][:, j, :], in_=xn[:, d : d + 1].to_broadcast([P, P]), identity=ident_f[:]
                 )
 
+        zh = const.tile([P, G * T * D], F32, name="zh")
+        nc.vector.tensor_scalar_mul(out=zh[:], in0=zf[:], scalar1=-0.5)
         kc = const.tile([P, G * T], F32, name="kc")
         exp_bias = {}
         for g in (0, 1):

@@ -51,6 +51,8 @@ def tile_tmk_w_kernel(tc, x, design_points, chol_inv_words, chol_inv_scales, out
                 out=z_sb[:],
                 in_=design_points.rearrange("(g p t) d -> p g (t d)", g=G, p=P, t=T),
             )
+        warm_src = const.tile([P, CHUNK], BF16, name="warm_src")
+        nc.vector.memset(warm_src[:], 0.0)
         w_scales = const.tile([P, 2, COLS], U8, name="w_scales", align_bytes=64)
         nc.vector.memset(w_scales[:].bitcast(I32), 0)
         for half in range(2):
@@ -68,16 +70,14 @@ def tile_tmk_w_kernel(tc, x, design_points, chol_inv_words, chol_inv_scales, out
             )
             w_words.append(wt)
 
-        warm_src = const.tile([P, CHUNK], BF16, name="warm_src")
-        nc.gpsimd.memset(warm_src[:], 0.0)
-        neg_half = const.tile([P, 1], F32, name="neg_half")
-        nc.gpsimd.memset(neg_half[:], -0.5)
         scratch = const.tile([P, 1], F32, name="scratch")
         nc.gpsimd.memset(scratch[:], 0.0)
-        scratch2 = const.tile([P, 1], F32, name="scratch2")
-        nc.scalar.activation(out=scratch2[:], in_=scratch[:], func=ACT.Exp)
+        neg_half = const.tile([P, 1], F32, name="neg_half")
+        nc.gpsimd.memset(neg_half[:], -0.5)
         ident_f = const.tile([P, P], F32, name="ident_f")
         make_identity(nc, ident_f[:])
+        scratch2 = const.tile([P, 1], F32, name="scratch2")
+        nc.scalar.activation(out=scratch2[:], in_=scratch[:], func=ACT.Exp)
 
         stats = const.tile([P, 6], F32, name="stats")
         nc.vector.bn_stats(out=stats[:], in_=x_sb[:])

from contextlib import ExitStack

import concourse.mybir as mybir
from concourse.masks import make_identity

F32 = mybir.dt.float32
BF16 = mybir.dt.bfloat16
I32 = mybir.dt.int32
U8 = mybir.dt.uint8
U32 = mybir.dt.uint32
FP8X4 = mybir.dt.float8_e4m3fn_x4
ACT = mybir.ActivationFunctionType
ALU = mybir.AluOpType
AX = mybir.AxisListType

P = 128
D = 16
G = 8
T = 4
COLS = 4096
CHUNK = 512
LN_EPS = 1e-5
S_OF_ROUND = (8, 7, 7, 6, 7, 6, 7, 6)
CUT_E = 8
CUT_C = 16
EARLY_CHUNKS = 6
MX_AFTER_FIRST = (4, 12, 20)
V_SPLIT = 28
PREWARM = 6

FLOPS = 2 * 128 * 4096 * 4096


def tile_tmk_w_kernel(tc, x, design_points, chol_inv_words, chol_inv_scales, out):
    nc = tc.nc
    with ExitStack() as ctx:
        ctx.enter_context(tc.manual_schedule())
        const = ctx.enter_context(tc.tile_pool(name="const", bufs=1))
        wpool = ctx.enter_context(tc.tile_pool(name="wpool", bufs=1))
        terms = ctx.enter_context(tc.tile_pool(name="terms", bufs=16))
        chains = ctx.enter_context(tc.tile_pool(name="chains", bufs=2))
        stage = ctx.enter_context(tc.tile_pool(name="stage", bufs=2))
        outp = ctx.enter_context(tc.tile_pool(name="outp", bufs=8))
        psum = ctx.enter_context(tc.psum_pool(name="psum", bufs=1))

        x_sb = const.tile([P, D], BF16, name="x_sb")
        nc.sync.dma_start(out=x_sb[:], in_=x)
        z_sb = const.tile([P, G, T * D], BF16, name="z_sb")
        with nc.allow_non_contiguous_dma(reason="128-byte runs of design points"):
            nc.sync.dma_start(
                out=z_sb[:],
                in_=design_points.rearrange("(g p t) d -> p g (t d)", g=G, p=P, t=T),
            )
        warm_src = const.tile([P, CHUNK], BF16, name="warm_src")
        nc.vector.memset(warm_src[:], 0.0)
        w_scales = const.tile([P, 2, COLS], U8, name="w_scales", align_bytes=64)
        nc.vector.memset(w_scales[:].bitcast(I32), 0)
        for half in range(2):
            for q in range(4):
                nc.sync.dma_start(
                    out=w_scales[32 * q : 32 * q + 16, half, :].bitcast(I32),
                    in_=chol_inv_scales[4 * half : 4 * half + 4, 4 * q : 4 * q + 4, :].bitcast(I32),
                )
        w_words = []
        for g in range(G):
            wt = wpool.tile([P, 4 * COLS], U8, name="w%d" % g, align_bytes=64)
            nc.sync.dma_start(
                out=wt[:].bitcast(I32),
                in_=chol_inv_words[g].rearrange("p n t -> p (n t)").bitcast(I32),
            )
            w_words.append(wt)

        scratch = const.tile([P, 1], F32, name="scratch")
        nc.gpsimd.memset(scratch[:], 0.0)
        neg_half = const.tile([P, 1], F32, name="neg_half")
        nc.gpsimd.memset(neg_half[:], -0.5)
        ident_f = const.tile([P, P], F32, name="ident_f")
        make_identity(nc, ident_f[:])
        scratch2 = const.tile([P, 1], F32, name="scratch2")
        nc.scalar.activation(out=scratch2[:], in_=scratch[:], func=ACT.Exp)

        stats = const.tile([P, 6], F32, name="stats")
        nc.vector.bn_stats(out=stats[:], in_=x_sb[:])
        mv = const.tile([P, 2], F32, name="mv")
        nc.vector.bn_aggr(out=mv[:], in_=stats[:])
        vare = const.tile([P, 1], F32, name="vare")
        nc.vector.tensor_scalar_add(out=vare[:], in0=mv[:, 1:2], scalar1=LN_EPS)
        rstd = const.tile([P, 1], F32, name="rstd")
        nc.gpsimd.tensor_tensor(out=rstd[:], in0=vare[:], in1=neg_half[:], op=ALU.pow)
        zf = const.tile([P, G * T * D], F32, name="zf")
        nc.vector.tensor_copy(out=zf[:], in_=z_sb[:].rearrange("p g k -> p (g k)"))
        xn = const.tile([P, D], F32, name="xn")
        nc.vector.tensor_scalar(
            out=xn[:], in0=x_sb[:], scalar1=mv[:, 0:1], scalar2=rstd[:], op0=ALU.subtract, op1=ALU.mult
        )

        xnb = const.tile([P, D, P], F32, name="xnb")
        warm = psum.tile([P, CHUNK], F32, tag="acc5", name="warm")

        def idle_matmuls(n):
            for i in range(n):
                nc.tensor.matmul(out=warm[:], lhsT=warm_src[:, 0:P], rhs=warm_src[:], start=True, stop=True)

        idle_matmuls(PREWARM)
        spread = {}
        for k in (0, 2, 1, 3):
            if k == 1:
                idle_matmuls(2)
            spread[k] = psum.tile([P, 4, P], F32, tag="acc%d" % k, name="bc%d" % k)
            for j in range(4):
                d = 4 * k + j
                nc.tensor.transpose(
                    out=spread[k][:, j, :], in_=xn[:, d : d + 1].to_broadcast([P, P]), identity=ident_f[:]
                )

        zh = const.tile([P, G * T * D], F32, name="zh")
        nc.vector.tensor_scalar_mul(out=zh[:], in0=zf[:], scalar1=-0.5)
        kc = const.tile([P, G * T], F32, name="kc")
        exp_bias = {}
        for g in (0, 1):
            nc.vector.tensor_reduce(
                out=kc[:, g * T : (g + 1) * T],
                in_=zh[:, g * T * D : (g + 1) * T * D].rearrange("p (b d) -> p b d", d=D)[:, :, S_OF_ROUND[g] : D],
                axis=AX.X,
                op=ALU.add,
            )
        for first in (2, 3):
            s = S_OF_ROUND[first]
            nc.vector.tensor_reduce(
                out=kc[:].rearrange("p (h two b) -> p h two b", two=2, b=T)[:, first // 2 : G // 2, first % 2, :],
                in_=zh[:].rearrange("p (h two b d) -> p h two b d", two=2, b=T, d=D)[
                    :, first // 2 : G // 2, first % 2, :, s:D
                ],
                axis=AX.X,
                op=ALU.add,
            )
        for s in sorted(set(S_OF_ROUND)):
            exp_bias[s] = const.tile([P, 1], F32, name="exp_bias%d" % s)
            nc.vector.tensor_reduce(out=exp_bias[s][:], in_=xn[:, s:D], axis=AX.X, op=ALU.add)
        nc.scalar.copy(out=xnb[:, 0:4, :], in_=spread[0][:])
        nc.vector.tensor_copy(out=xnb[:, 8:12, :], in_=spread[2][:])

        kcodes = const.tile([P, G, P], U32, name="kcodes", align_bytes=64)
        kscales = const.tile([P, G, P], U8, name="kscales", align_bytes=64)

        work_tags = ("wka", "wkb")
        v_dims = [[d for d in range(8, D)] + [d for d in range(s, 8)] for s in S_OF_ROUND]
        acc = {}
        l1 = {}
        sums = {}
        kn = {}
        xt = {}
        grouped = {}
        opened = {}
        t_count = [0]
        points = [MX_AFTER_FIRST]
        pending = []
        late = []
        pos = [0, 0]

        def mx_pass(c, g):
            k4 = 4 * (g % 4)
            nc.tensor.matmul_mx(
                out=acc[c][:],
                lhsT=kcodes[:, g, :].bitcast(FP8X4),
                lhsT_scale=kscales[:, g, :],
                rhs=w_words[g][:, 4 * CHUNK * c : 4 * CHUNK * (c + 1)].bitcast(FP8X4),
                rhs_scale=w_scales[k4:P, g // 4, CHUNK * c : CHUNK * (c + 1)],
                start=(g == 0),
                stop=(g == G - 1),
            )

        def emit_passes(n):
            for i in range(n):
                if pos[0] < len(pending):
                    c, g = pending[pos[0]]
                    pos[0] += 1
                    mx_pass(c, g)
                elif pos[1] < len(late):
                    c, g = late[pos[1]]
                    pos[1] += 1
                    mx_pass(c, g)
                elif len(pending) == 0:
                    idle_matmuls(1)

        def after_t():
            t_count[0] += 1
            if t_count[0] in points[0]:
                emit_passes(2)

        def add_transposed(g, t, src, last):
            nc.tensor.matmul(
                out=l1[g][:, t * P : (t + 1) * P],
                lhsT=src,
                rhs=ident_f[:],
                is_transpose=True,
                start=(g not in opened),
                stop=last,
            )
            opened[g] = True
            after_t()

        def scalar_terms(g, pairs):
            for t, d in pairs:
                b = g * T + t
                term = terms.tile([P, P], F32, tag="term", name="term")
                nc.scalar.activation(
                    out=term[:],
                    in_=xnb[:, d, :],
                    func=ACT.Abs,
                    bias=zh[:, b * D + d : b * D + d + 1],
                    scale=0.5,
                )
                add_transposed(g, t, term[:], False)

        def vector_ops(g, lo, hi):
            for k, t in [(k, t) for k in range(len(v_dims[g])) for t in range(T)][lo:hi]:
                d = v_dims[g][k]
                b = g * T + t
                if k == 0:
                    sums[(g, t)] = chains.tile([P, P], F32, tag="sum%d" % t, name="sum%d" % t)
                    nc.vector.tensor_scalar(
                        out=sums[(g, t)][:],
                        in0=xnb[:, d, :],
                        scalar1=zf[:, b * D + d : b * D + d + 1],
                        scalar2=kc[:, b : b + 1],
                        op0=ALU.max,
                        op1=ALU.add,
                    )
                else:
                    nc.vector.scalar_tensor_tensor(
                        out=sums[(g, t)][:],
                        in0=xnb[:, d, :],
                        scalar=zf[:, b * D + d : b * D + d + 1],
                        in1=sums[(g, t)][:],
                        op0=ALU.max,
                        op1=ALU.add,
                    )

        def vector_sums_in(g):
            for t in range(T):
                add_transposed(g, t, sums[(g, t)][:], t == T - 1)

        def exponent(g):
            kn[g] = stage.tile([P, 2, P, 2], BF16, tag="kn", name="kn")
            nc.scalar.activation(
                out=kn[g][:],
                in_=l1[g][:].rearrange("n (u e p) -> n u p e", u=2, e=2),
                func=ACT.Exp,
                bias=exp_bias[S_OF_ROUND[g]][:],
                scale=-2.0,
            )

        def turn_back(g):
            xt[g] = psum.tile([P, 2, P], F32, tag=work_tags[g % 2], name="xt_%d" % g)
            words = kn[g][:].rearrange("n u p e -> n (u p e)").bitcast(F32)
            for u in range(2):
                nc.tensor.transpose(out=xt[g][:, u, :], in_=words[:, u * P : (u + 1) * P], identity=ident_f[:])
                after_t()

        def regroup(g):
            grouped[g] = stage.tile([P, P, T], BF16, tag="grouped", name="grouped", align_bytes=64)
            nc.scalar.copy(
                out=grouped[g][:].rearrange("p n t -> p (n t)").bitcast(F32).rearrange("p (n u) -> p n u", u=2),
                in_=xt[g][:].rearrange("p u n -> p n u"),
            )

        def quantise(g):
            nc.vector.quantize_mx(
                out=kcodes[:, g, :].bitcast(FP8X4),
                scales=kscales[:, g, :],
                in_=grouped[g][:].rearrange("p n t -> p (n t)"),
            )

        def evacuate(c):
            res = outp.tile([P, CHUNK], F32, tag="res", name="res%d" % c)
            if c % 2 == 0:
                nc.vector.tensor_copy(out=res[:], in_=acc[c][:])
                nc.sync.dma_start(out=out[:, CHUNK * c : CHUNK * (c + 1)], in_=res[:])
            else:
                nc.scalar.copy(out=res[:], in_=acc[c][:])
                nc.scalar.dma_start(out=out[:, CHUNK * c : CHUNK * (c + 1)], in_=res[:])

        for g in range(G):
            n_vops = T * len(v_dims[g])
            order = [(t, d) for d in range(S_OF_ROUND[g]) for t in range(T)]
            n_turns = T + len(order) + 2
            t_count[0] = 0
            points[0] = tuple(6 + (n_turns * i) // 3 for i in range(3)) if g > 0 else MX_AFTER_FIRST
            l1[g] = psum.tile([P, T * P], F32, tag=work_tags[g % 2], name="l1_%d" % g)
            if g == 0:
                scalar_terms(g, order[0:16])
                nc.scalar.copy(out=xnb[:, 4:8, :], in_=spread[1][:])
                vector_ops(g, 0, 16)
                nc.vector.tensor_copy(out=xnb[:, 12:16, :], in_=spread[3][:])
                vector_ops(g, 16, V_SPLIT)
                scalar_terms(g, order[16:])
            else:
                vector_sums_in(g - 1)
                scalar_terms(g, order[0:CUT_E])
                exponent(g - 1)
                turn_back(g - 1)
                scalar_terms(g, order[CUT_E:CUT_C])
                regroup(g - 1)
                if g - 1 == G - 2:
                    acc[6] = psum.tile([P, CHUNK], F32, tag=work_tags[(g - 1) % 2], name="out6")
                    for gg in range(G - 2):
                        late.append((6, gg))
                vector_ops(g, 0, V_SPLIT)
                quantise(g - 1)
                if g - 1 == 0:
                    for c in range(EARLY_CHUNKS):
                        acc[c] = psum.tile([P, CHUNK], F32, tag="acc%d" % c, name="out%d" % c)
                for c in range(EARLY_CHUNKS):
                    pending.append((c, g - 1))
                if g - 1 == G - 2:
                    late.append((6, g - 1))
                scalar_terms(g, order[CUT_C:])
            vector_ops(g, V_SPLIT, n_vops)

        g = G - 1
        t_count[0] = 100
        vector_sums_in(g)
        emit_passes(4)
        exponent(g)
        turn_back(g)
        emit_passes(6)
        regroup(g)
        quantise(g)
        for c in range(EARLY_CHUNKS):
            pending.append((c, g))
        late.append((6, g))
        emit_passes(len(pending) - pos[0])
        for c in range(EARLY_CHUNKS):
            evacuate(c)
        emit_passes(len(late) - pos[1])
        evacuate(6)
        half = CHUNK // 2
        for h, tag in enumerate((work_tags[g % 2], "acc0")):
            part = psum.tile([P, half], F32, tag=tag, name="out7_%d" % h)
            lo = CHUNK * 7 + half * h
            for gg in range(G):
                nc.tensor.matmul_mx(
                    out=part[:],
                    lhsT=kcodes[:, gg, :].bitcast(FP8X4),
                    lhsT_scale=kscales[:, gg, :],
                    rhs=w_words[gg][:, 4 * lo : 4 * (lo + half)].bitcast(FP8X4),
                    rhs_scale=w_scales[4 * (gg % 4) : P, gg // 4, lo : lo + half],
                    start=(gg == 0),
                    stop=(gg == G - 1),
                )
            res = outp.tile([P, half], F32, tag="res", name="res7_%d" % h)
            if h == 0:
                nc.vector.tensor_copy(out=res[:], in_=part[:])
                nc.sync.dma_start(out=out[:, lo : lo + half], in_=res[:])
            else:
                nc.scalar.copy(out=res[:], in_=part[:])
                nc.scalar.dma_start(out=out[:, lo : lo + half], in_=res[:])
